import numpy as np
import ml_dtypes


def mxq(x, axis, fmt="e4m3"):
    dtype, down = {"e4m3": (ml_dtypes.float8_e4m3fn, 7), "e5m2": (ml_dtypes.float8_e5m2, 14)}[fmt]
    v = np.moveaxis(np.asarray(x, np.float32).astype(ml_dtypes.bfloat16).astype(np.float64), axis, -1)
    blocks = v.reshape(v.shape[:-1] + (-1, 32))
    amax = np.abs(blocks).max(-1, keepdims=True)
    byte = np.maximum(np.where(amax > 0, np.frexp(amax)[1] - 1 + 127, 0) - down, 1)
    scale = np.exp2(byte - 127.0)
    codes = (blocks / scale).astype(np.float32).astype(dtype).astype(np.float64)
    return np.moveaxis((codes * scale).reshape(v.shape), -1, axis)


WIDE = False


def mx_kscale(k):
    if not WIDE:
        return np.ones(k)
    levels = np.array([10, -10, 5, -5, 0])
    if k % 512:
        return np.exp2(np.random.permutation(np.resize(levels, k // 32))).repeat(32)
    a = np.empty((k // 512, 16))
    for p in range(k // 512):
        a[p, :8] = np.random.permutation(np.resize(levels, 8))
        for g in range(8):
            far = levels[np.abs(levels - a[p, g]) >= 10]
            a[p, g + 8] = far[np.random.randint(len(far))]
    return np.exp2(a.ravel()).repeat(32)


BF16 = ml_dtypes.bfloat16


def bf(x):
    return np.asarray(x, np.float32).astype(BF16)


def f64(x):
    return np.asarray(x).astype(np.float64)


B, S, D = 128, 16, 512


def sigmoid(v):
    return 1.0 / (1.0 + np.exp(-v))


def setup_inputs():
    s, t = mx_kscale(D), mx_kscale(D)
    return {
        "inputs": bf(np.random.standard_normal((B, D)) * s),
        "h_state": bf((np.random.standard_normal((B, S, D)) * 0.5 * t).reshape(B, S * D)),
        "c_state": bf(np.random.standard_normal((B, S * D)) * 0.5),
        "c_upd": bf(np.random.standard_normal((B, S, D))),
        "kernel": bf(np.random.standard_normal((D, 3 * D)) / np.sqrt(D) / s[:, None]),
        "recurrent_kernel": bf(np.random.standard_normal((D, 3 * D)) / np.sqrt(D) / t[:, None]),
        "bias": bf(np.random.standard_normal(3 * D) * 0.3),
    }


def reference(inputs, h_state, c_state, c_upd, kernel, recurrent_kernel, bias):
    h_tm1 = f64(h_state).reshape(B, S, D)
    c_tm1 = f64(c_state).reshape(B, S, D)
    xz = mxq(f64(inputs), 1, "e4m3") @ mxq(f64(kernel), 0, "e4m3")
    hz = mxq(h_tm1, 2, "e4m3") @ mxq(f64(recurrent_kernel), 0, "e4m3")
    z = xz[:, None, :] + hz + f64(bias)
    i = sigmoid(z[..., :D])
    f = sigmoid(z[..., D:2 * D])
    o = sigmoid(z[..., 2 * D:])
    c_new = f * c_tm1 + i * np.tanh(f64(c_upd))
    h_new = o * np.tanh(c_new)
    return h_new.reshape(B, -1), c_new.reshape(B, -1)

@@ -1,0 +1,291 @@
+from contextlib import ExitStack
+
+import concourse.mybir as mybir
+from concourse.masks import make_identity
+
+F32 = mybir.dt.float32
+BF16 = mybir.dt.bfloat16
+U32 = mybir.dt.uint32
+U8 = mybir.dt.uint8
+FP8X4 = mybir.dt.float8_e4m3fn_x4
+SIGMOID = mybir.ActivationFunctionType.Sigmoid
+TANH = mybir.ActivationFunctionType.Tanh
+MULT = mybir.AluOpType.mult
+ADD = mybir.AluOpType.add
+
+P = 128
+BATCH = 128
+SLOTS = 16
+D = 512
+GATES = 3
+PACK = 4
+HALVES = 2
+GROUP = 4
+GROUPS = SLOTS // GROUP
+BLOCKS = D // P
+MOVING = GROUP * BATCH
+
+FLOPS = 2 * (BATCH + BATCH * SLOTS) * D * GATES * D
+
+
+def tile_rlstmcell_pb_kernel(
+    tc, inputs, h_state, c_state, c_upd, kernel, recurrent_kernel, bias, out_0, out_1
+):
+    nc = tc.nc
+    with ExitStack() as ctx:
+        const = ctx.enter_context(tc.tile_pool(name="const", bufs=1))
+        resident = ctx.enter_context(tc.tile_pool(name="resident", bufs=1))
+        stage = ctx.enter_context(tc.tile_pool(name="stage", bufs=2))
+        gate_pool = ctx.enter_context(tc.tile_pool(name="gate_pool", bufs=2 * BLOCKS))
+        work = ctx.enter_context(tc.tile_pool(name="work", bufs=2))
+        z_psum = ctx.enter_context(tc.psum_pool(name="z_psum", bufs=4))
+        t_psum = ctx.enter_context(tc.psum_pool(name="t_psum", bufs=4))
+
+        weights = {"r": recurrent_kernel, "k": kernel}
+        w_raw, h_sb, c_sb, cu_sb = {}, {}, {}, {}
+
+        def load_weights(g):
+            for w in ("r", "k"):
+                w_raw[(w, g)] = resident.tile([P, PACK, D], BF16, name="raw_%s%d" % (w, g))
+                nc.sync.dma_start(
+                    out=w_raw[(w, g)][:],
+                    in_=weights[w][:, g * D : (g + 1) * D].rearrange("(p t) c -> p t c", t=PACK),
+                )
+
+        def load_h(t):
+            h_sb[t] = resident.tile([P, GROUP * D], BF16, name="h_sb%d" % t)
+            nc.sync.dma_start(out=h_sb[t][:], in_=h_state[:, t * GROUP * D : (t + 1) * GROUP * D])
+
+        def load_candidate(t):
+            cu_sb[t] = resident.tile([P, GROUP, D], BF16, name="cu_sb%d" % t)
+            nc.sync.dma_start(out=cu_sb[t][:], in_=c_upd[:, t * GROUP : (t + 1) * GROUP, :])
+
+        def load_cell(t):
+            c_sb[t] = resident.tile([P, GROUP, D], BF16, name="c_sb%d" % t)
+            nc.sync.dma_start(
+                out=c_sb[t][:],
+                in_=c_state[:, t * GROUP * D : (t + 1) * GROUP * D].rearrange(
+                    "b (s d) -> b s d", s=GROUP
+                ),
+            )
+
+        bias_rows = const.tile([P, P], BF16, name="bias_rows")
+        nc.vector.memset(bias_rows[:], 0.0)
+        nc.scalar.dma_start(
+            out=bias_rows[0 : GATES * BLOCKS, :], in_=bias.rearrange("(m p) -> m p", p=P)
+        )
+
+        x_sb = resident.tile([P, D], BF16, name="x_sb")
+        nc.sync.dma_start(out=x_sb[:], in_=inputs)
+        load_h(0)
+        load_weights(0)
+        load_weights(1)
+        load_h(1)
+        load_candidate(0)
+        load_weights(2)
+        load_cell(0)
+        for t in range(1, GROUPS):
+            if t + 1 < GROUPS:
+                load_h(t + 1)
+            load_candidate(t)
+            load_cell(t)
+
+        warm = const.tile([P, 1], F32, name="warm")
+        nc.vector.memset(warm[:], 0.0)
+        nc.scalar.activation(out=warm[:], in_=warm[:], func=SIGMOID)
+
+        ident = const.tile([P, P], F32, name="ident")
+        make_identity(nc, ident[:])
+
+        xT_ps = t_psum.tile([P, MOVING], F32, name="xT_ps", tag="t")
+        x_words = x_sb[:].bitcast(F32)
+        for u in range(HALVES):
+            nc.tensor.transpose(
+                xT_ps[:, u * P : (u + 1) * P], x_words[:, u : HALVES * P : HALVES], ident[:]
+            )
+        xT_grouped = resident.tile([P, MOVING * PACK], BF16, name="xT_grouped", align_bytes=64)
+        nc.scalar.copy(
+            out=xT_grouped[:].bitcast(F32).rearrange("p (s b u) -> p s b u", s=GROUP, u=HALVES),
+            in_=xT_ps[:, 0 : HALVES * P]
+            .rearrange("p (u b) -> p b u", u=HALVES)
+            .unsqueeze(1)
+            .to_broadcast([P, GROUP, BATCH, HALVES]),
+        )
+        xT_codes = resident.tile([P, MOVING], U32, name="xT_codes", align_bytes=64)
+        xT_scales = resident.tile([P, MOVING], U8, name="xT_scales", align_bytes=64)
+
+        bias_rows_f32 = const.tile([P, P], F32, name="bias_rows_f32")
+        nc.vector.tensor_copy(out=bias_rows_f32[:], in_=bias_rows[:])
+        bias_ps = t_psum.tile([P, MOVING], F32, name="bias_ps", tag="t")
+        nc.tensor.transpose(bias_ps[:, 0:P], bias_rows_f32[:], ident[:])
+        bias_cols = const.tile([P, GATES * BLOCKS], F32, name="bias_cols")
+        nc.scalar.copy(out=bias_cols[:], in_=bias_ps[:, 0 : GATES * BLOCKS])
+
+        hT_grouped, hT_codes, hT_scales = {}, {}, {}
+
+        def transpose_h(t, pair, copy):
+            if pair == 0:
+                hT_grouped[t] = stage.tile(
+                    [P, MOVING * PACK], BF16, name="hT_grouped", align_bytes=64
+                )
+            h_words = h_sb[t][:].bitcast(F32)
+            hT_ps = t_psum.tile([P, MOVING], F32, name="hT_ps", tag="t")
+            for u in range(HALVES):
+                for j in range(2):
+                    slot = (2 * pair + j) * HALVES * P
+                    nc.tensor.transpose(
+                        hT_ps[:, (2 * u + j) * P : (2 * u + j + 1) * P],
+                        h_words[:, slot + u : slot + HALVES * P : HALVES],
+                        ident[:],
+                    )
+            copy(
+                out=hT_grouped[t][:]
+                .bitcast(F32)[:, pair * MOVING : (pair + 1) * MOVING]
+                .rearrange("p (c u) -> p c u", u=HALVES),
+                in_=hT_ps[:].rearrange("p (u c) -> p c u", u=HALVES),
+            )
+
+        def quantise_h(t):
+            hT_codes[t] = stage.tile([P, MOVING], U32, name="hT_codes", align_bytes=64)
+            hT_scales[t] = stage.tile([P, MOVING], U8, name="hT_scales", align_bytes=64)
+            nc.vector.quantize_mx(
+                out=hT_codes[t][:].bitcast(FP8X4), scales=hT_scales[t][:], in_=hT_grouped[t][:]
+            )
+
+        w_grouped = {}
+        w_codes = {w: resident.tile([P, GATES * D], U32, name="codes_" + w, align_bytes=64) for w in weights}
+        w_scales = {w: resident.tile([P, GATES * D], U8, name="scales_" + w, align_bytes=64) for w in weights}
+
+        def regroup_weights(g):
+            for w in ("r", "k"):
+                w_grouped[w] = stage.tile([P, D, PACK], BF16, name="grouped_" + w, align_bytes=64)
+                nc.vector.tensor_copy(
+                    out=w_grouped[w][:].rearrange("p (c i) t -> p c t i", i=4),
+                    in_=w_raw[(w, g)][:].rearrange("p t (c i) -> p c t i", i=4),
+                )
+
+        def quantise_weights(g):
+            for w in ("r", "k"):
+                nc.vector.quantize_mx(
+                    out=w_codes[w][:, g * D : (g + 1) * D].bitcast(FP8X4),
+                    scales=w_scales[w][:, g * D : (g + 1) * D],
+                    in_=w_grouped[w][:].rearrange("p c t -> p (c t)"),
+                )
+
+        def block(tile3, q):
+            return tile3[:, :, q * P : (q + 1) * P]
+
+        def preactivation(t, g, q):
+            cols = slice((g * BLOCKS + q) * P, (g * BLOCKS + q + 1) * P)
+            z = z_psum.tile([P, MOVING], F32, name="z")
+            nc.tensor.matmul_mx(
+                out=z[:],
+                lhsT=w_codes["r"][:, cols].bitcast(FP8X4),
+                lhsT_scale=w_scales["r"][:, cols],
+                rhs=hT_codes[t][:].bitcast(FP8X4),
+                rhs_scale=hT_scales[t][:],
+                start=True,
+                stop=False,
+            )
+            nc.tensor.matmul_mx(
+                out=z[:],
+                lhsT=w_codes["k"][:, cols].bitcast(FP8X4),
+                lhsT_scale=w_scales["k"][:, cols],
+                rhs=xT_codes[:].bitcast(FP8X4),
+                rhs_scale=xT_scales[:],
+                start=False,
+                stop=True,
+            )
+            return z
+
+        def sigmoid(z, g, q):
+            gateT = gate_pool.tile([P, MOVING], F32, name="gateT")
+            m = g * BLOCKS + q
+            nc.scalar.activation(
+                out=gateT[:], in_=z[:], func=SIGMOID, bias=bias_cols[:, m : m + 1], scale=1.0
+            )
+            return gateT
+
+        def to_batch_rows(gateT):
+            gate = t_psum.tile([P, GROUP * P], F32, name="gate", tag="t")
+            for s in range(GROUP):
+                nc.tensor.transpose(gate[:, s * P : (s + 1) * P], gateT[:, s * P : (s + 1) * P], ident[:])
+            return gate[:].rearrange("b (s d) -> b s d", s=GROUP)
+
+        cand, keep, c_new, tanh_c, h_new = {}, {}, {}, {}, {}
+
+        def tanh_candidate(t, first_slot, slots):
+            if first_slot == 0:
+                cand[t] = work.tile([P, GROUP, D], F32, name="cand")
+            part = slice(first_slot, first_slot + slots)
+            nc.scalar.activation(out=cand[t][:, part, :], in_=cu_sb[t][:, part, :], func=TANH)
+
+        def apply_gate(t, g, q, gate):
+            if g == 0:
+                nc.vector.tensor_tensor(out=block(cand[t], q), in0=gate, in1=block(cand[t], q), op=MULT)
+            if g == 1:
+                if q == 0:
+                    keep[t] = work.tile([P, GROUP, D], F32, name="keep")
+                    c_new[t] = work.tile([P, GROUP, D], F32, name="c_new")
+                nc.vector.tensor_tensor(out=block(keep[t], q), in0=gate, in1=block(c_sb[t], q), op=MULT)
+                nc.gpsimd.tensor_tensor(
+                    out=block(c_new[t], q), in0=block(keep[t], q), in1=block(cand[t], q), op=ADD
+                )
+            if g == 2:
+                if q == 0:
+                    h_new[t] = work.tile([P, GROUP, D], F32, name="h_new")
+                nc.vector.tensor_tensor(out=block(h_new[t], q), in0=gate, in1=block(tanh_c[t], q), op=MULT)
+
+        def tanh_cell(t, q):
+            if q == 0:
+                tanh_c[t] = work.tile([P, GROUP, D], F32, name="tanh_c")
+            nc.scalar.activation(out=block(tanh_c[t], q), in_=block(c_new[t], q), func=TANH)
+
+        def store(out, t, tile3):
+            nc.sync.dma_start(
+                out=out[:, t * GROUP * D : (t + 1) * GROUP * D],
+                in_=tile3[:].rearrange("b s d -> b (s d)"),
+            )
+
+        transpose_h(0, 0, nc.scalar.copy)
+        transpose_h(0, 1, nc.scalar.copy)
+        nc.vector.quantize_mx(out=xT_codes[:].bitcast(FP8X4), scales=xT_scales[:], in_=xT_grouped[:])
+        regroup_weights(0)
+        quantise_h(0)
+        quantise_weights(0)
+
+        rounds = [(t, g) for t in range(GROUPS) for g in range(GATES)]
+        gatesT = {}
+        for r in range(len(rounds) + 1):
+            if r < len(rounds):
+                t, g = rounds[r]
+                zs = [preactivation(t, g, q) for q in range(BLOCKS)]
+                if t == 0 and g + 1 < GATES:
+                    regroup_weights(g + 1)
+                    quantise_weights(g + 1)
+                for q in range(BLOCKS):
+                    gatesT[(r, q)] = sigmoid(zs[q], g, q)
+                    if g == 0 and t > 0:
+                        tanh_cell(t - 1, q)
+                if r == 0:
+                    tanh_candidate(0, 0, GROUP)
+                if g > 0 and t + 1 < GROUPS:
+                    tanh_candidate(t + 1, (g - 1) * 2, 2)
+            else:
+                for q in range(BLOCKS):
+                    tanh_cell(GROUPS - 1, q)
+            if r > 0:
+                t_done, g_done = rounds[r - 1]
+                for q in range(BLOCKS):
+                    apply_gate(t_done, g_done, q, to_batch_rows(gatesT[(r - 1, q)]))
+                if g_done == 1:
+                    store(out_1, t_done, c_new[t_done])
+                if g_done == 2:
+                    store(out_0, t_done, h_new[t_done])
+            if r < len(rounds):
+                t, g = rounds[r]
+                if t + 1 < GROUPS:
+                    if g < 2:
+                        transpose_h(t + 1, g, nc.vector.tensor_copy)
+                    else:
+                        quantise_h(t + 1)

@@ -17,6 +17,7 @@ P = 128
 BATCH = 128
 SLOTS = 16
 D = 512
+I, F, O = 0, 1, 2
 GATES = 3
 PACK = 4
 HALVES = 2
@@ -35,33 +36,35 @@ def tile_rlstmcell_pb_kernel(
     with ExitStack() as ctx:
         const = ctx.enter_context(tc.tile_pool(name="const", bufs=1))
         resident = ctx.enter_context(tc.tile_pool(name="resident", bufs=1))
+        loads = ctx.enter_context(tc.tile_pool(name="loads", bufs=3))
         stage = ctx.enter_context(tc.tile_pool(name="stage", bufs=2))
         gate_pool = ctx.enter_context(tc.tile_pool(name="gate_pool", bufs=2 * BLOCKS))
+        block_pool = ctx.enter_context(tc.tile_pool(name="block_pool", bufs=BLOCKS))
         work = ctx.enter_context(tc.tile_pool(name="work", bufs=2))
         z_psum = ctx.enter_context(tc.psum_pool(name="z_psum", bufs=4))
         t_psum = ctx.enter_context(tc.psum_pool(name="t_psum", bufs=4))
+        ctx.enter_context(tc.manual_schedule())
 
         weights = {"r": recurrent_kernel, "k": kernel}
         w_raw, h_sb, c_sb, cu_sb = {}, {}, {}, {}
 
-        def load_weights(g):
-            for w in ("r", "k"):
-                w_raw[(w, g)] = resident.tile([P, PACK, D], BF16, name="raw_%s%d" % (w, g))
-                nc.sync.dma_start(
-                    out=w_raw[(w, g)][:],
-                    in_=weights[w][:, g * D : (g + 1) * D].rearrange("(p t) c -> p t c", t=PACK),
-                )
+        def load_weights(w, g):
+            w_raw[(w, g)] = loads.tile([P, PACK, D], BF16, name="raw_" + w, bufs=2)
+            nc.sync.dma_start(
+                out=w_raw[(w, g)][:],
+                in_=weights[w][:, g * D : (g + 1) * D].rearrange("(p t) c -> p t c", t=PACK),
+            )
 
         def load_h(t):
-            h_sb[t] = resident.tile([P, GROUP * D], BF16, name="h_sb%d" % t)
+            h_sb[t] = loads.tile([P, GROUP * D], BF16, name="h_rows")
             nc.sync.dma_start(out=h_sb[t][:], in_=h_state[:, t * GROUP * D : (t + 1) * GROUP * D])
 
         def load_candidate(t):
-            cu_sb[t] = resident.tile([P, GROUP, D], BF16, name="cu_sb%d" % t)
+            cu_sb[t] = loads.tile([P, GROUP, D], BF16, name="candidate_rows")
             nc.sync.dma_start(out=cu_sb[t][:], in_=c_upd[:, t * GROUP : (t + 1) * GROUP, :])
 
         def load_cell(t):
-            c_sb[t] = resident.tile([P, GROUP, D], BF16, name="c_sb%d" % t)
+            c_sb[t] = loads.tile([P, GROUP, D], BF16, name="cell_rows")
             nc.sync.dma_start(
                 out=c_sb[t][:],
                 in_=c_state[:, t * GROUP * D : (t + 1) * GROUP * D].rearrange(
@@ -71,24 +74,38 @@ def tile_rlstmcell_pb_kernel(
 
         bias_rows = const.tile([P, P], BF16, name="bias_rows")
         nc.vector.memset(bias_rows[:], 0.0)
-        nc.scalar.dma_start(
-            out=bias_rows[0 : GATES * BLOCKS, :], in_=bias.rearrange("(m p) -> m p", p=P)
+        bias_row = const.tile([P, D], BF16, name="bias_row")
+        nc.vector.memset(bias_row[:], 0.0)
+        ones = const.tile([P, P], BF16, name="ones")
+        nc.vector.memset(ones[:], 1.0)
+        nc.sync.dma_start(
+            out=bias_rows[0 : (GATES - 1) * BLOCKS, :],
+            in_=bias[D : GATES * D].rearrange("(m p) -> m p", p=P),
+        )
+        nc.sync.dma_start(
+            out=bias_row[0:1, :], in_=bias[0:D].rearrange("(m p) -> m p", p=D)
         )
 
+        load_weights("r", F)
         x_sb = resident.tile([P, D], BF16, name="x_sb")
         nc.sync.dma_start(out=x_sb[:], in_=inputs)
         load_h(0)
-        load_weights(0)
-        load_weights(1)
-        load_h(1)
+        load_weights("k", F)
         load_candidate(0)
-        load_weights(2)
+        load_h(1)
+        load_weights("r", I)
+        load_weights("k", I)
+        load_candidate(1)
         load_cell(0)
-        for t in range(1, GROUPS):
-            if t + 1 < GROUPS:
-                load_h(t + 1)
-            load_candidate(t)
-            load_cell(t)
+        load_weights("r", O)
+        load_weights("k", O)
+        load_candidate(2)
+        load_h(2)
+        load_cell(1)
+        load_candidate(3)
+        load_h(3)
+        load_cell(2)
+        load_cell(3)
 
         warm = const.tile([P, 1], F32, name="warm")
         nc.vector.memset(warm[:], 0.0)
@@ -97,29 +114,40 @@ def tile_rlstmcell_pb_kernel(
         ident = const.tile([P, P], F32, name="ident")
         make_identity(nc, ident[:])
 
-        xT_ps = t_psum.tile([P, MOVING], F32, name="xT_ps", tag="t")
-        x_words = x_sb[:].bitcast(F32)
-        for u in range(HALVES):
-            nc.tensor.transpose(
-                xT_ps[:, u * P : (u + 1) * P], x_words[:, u : HALVES * P : HALVES], ident[:]
-            )
-        xT_grouped = resident.tile([P, MOVING * PACK], BF16, name="xT_grouped", align_bytes=64)
-        nc.scalar.copy(
-            out=xT_grouped[:].bitcast(F32).rearrange("p (s b u) -> p s b u", s=GROUP, u=HALVES),
-            in_=xT_ps[:, 0 : HALVES * P]
-            .rearrange("p (u b) -> p b u", u=HALVES)
-            .unsqueeze(1)
-            .to_broadcast([P, GROUP, BATCH, HALVES]),
-        )
         xT_codes = resident.tile([P, MOVING], U32, name="xT_codes", align_bytes=64)
         xT_scales = resident.tile([P, MOVING], U8, name="xT_scales", align_bytes=64)
+        xT_grouped = resident.tile([P, BATCH * PACK], BF16, name="xT_grouped", align_bytes=64)
 
-        bias_rows_f32 = const.tile([P, P], F32, name="bias_rows_f32")
-        nc.vector.tensor_copy(out=bias_rows_f32[:], in_=bias_rows[:])
-        bias_ps = t_psum.tile([P, MOVING], F32, name="bias_ps", tag="t")
-        nc.tensor.transpose(bias_ps[:, 0:P], bias_rows_f32[:], ident[:])
-        bias_cols = const.tile([P, GATES * BLOCKS], F32, name="bias_cols")
-        nc.scalar.copy(out=bias_cols[:], in_=bias_ps[:, 0 : GATES * BLOCKS])
+        def transpose_x():
+            xT_ps = t_psum.tile([P, MOVING], F32, name="xT_ps", tag="t")
+            x_words = x_sb[:].bitcast(F32)
+            for u in range(HALVES):
+                nc.tensor.transpose(
+                    xT_ps[:, u * P : (u + 1) * P], x_words[:, u : HALVES * P : HALVES], ident[:]
+                )
+            nc.scalar.copy(
+                out=xT_grouped[:].bitcast(F32).rearrange("p (b u) -> p b u", u=HALVES),
+                in_=xT_ps[:, 0 : HALVES * P].rearrange("p (u b) -> p b u", u=HALVES),
+            )
+
+        def quantise_x(s):
+            cols = slice(s * BATCH, (s + 1) * BATCH)
+            nc.vector.quantize_mx(
+                out=xT_codes[:, cols].bitcast(FP8X4), scales=xT_scales[:, cols], in_=xT_grouped[:]
+            )
+
+        bias_cols = const.tile([P, (GATES - 1) * BLOCKS], F32, name="bias_cols")
+        bias_i = const.tile([P, D], F32, name="bias_i")
+
+        def spread_biases():
+            bias_rows_f32 = const.tile([P, P], F32, name="bias_rows_f32")
+            nc.vector.tensor_copy(out=bias_rows_f32[:], in_=bias_rows[:])
+            bias_ps = t_psum.tile([P, MOVING], F32, name="bias_ps", tag="t")
+            nc.tensor.transpose(bias_ps[:, 0:P], bias_rows_f32[:], ident[:])
+            nc.scalar.copy(out=bias_cols[:], in_=bias_ps[:, 0 : (GATES - 1) * BLOCKS])
+            spread = t_psum.tile([P, D], F32, name="spread", tag="t")
+            nc.tensor.matmul(spread[:], lhsT=ones[:], rhs=bias_row[:], start=True, stop=True)
+            nc.scalar.copy(out=bias_i[:], in_=spread[:])
 
         hT_grouped, hT_codes, hT_scales = {}, {}, {}
 
@@ -156,26 +184,50 @@ def tile_rlstmcell_pb_kernel(
         w_codes = {w: resident.tile([P, GATES * D], U32, name="codes_" + w, align_bytes=64) for w in weights}
         w_scales = {w: resident.tile([P, GATES * D], U8, name="scales_" + w, align_bytes=64) for w in weights}
 
-        def regroup_weights(g):
-            for w in ("r", "k"):
-                w_grouped[w] = stage.tile([P, D, PACK], BF16, name="grouped_" + w, align_bytes=64)
-                nc.vector.tensor_copy(
-                    out=w_grouped[w][:].rearrange("p (c i) t -> p c t i", i=4),
-                    in_=w_raw[(w, g)][:].rearrange("p t (c i) -> p c t i", i=4),
-                )
+        def regroup_weights(w, g, copy):
+            w_grouped[w] = stage.tile([P, D, PACK], BF16, name="grouped_" + w, align_bytes=64)
+            copy(
+                out=w_grouped[w][:].rearrange("p (c i) t -> p c t i", i=4),
+                in_=w_raw[(w, g)][:].rearrange("p t (c i) -> p c t i", i=4),
+            )
 
-        def quantise_weights(g):
-            for w in ("r", "k"):
-                nc.vector.quantize_mx(
-                    out=w_codes[w][:, g * D : (g + 1) * D].bitcast(FP8X4),
-                    scales=w_scales[w][:, g * D : (g + 1) * D],
-                    in_=w_grouped[w][:].rearrange("p c t -> p (c t)"),
-                )
+        def quantise_weights(w, g):
+            nc.vector.quantize_mx(
+                out=w_codes[w][:, g * D : (g + 1) * D].bitcast(FP8X4),
+                scales=w_scales[w][:, g * D : (g + 1) * D],
+                in_=w_grouped[w][:].rearrange("p c t -> p (c t)"),
+            )
 
-        def block(tile3, q):
-            return tile3[:, :, q * P : (q + 1) * P]
+        def h_stationary(t, s):
+            z = z_psum.tile([P, D], F32, name="z")
+            rows = slice(s * BATCH, (s + 1) * BATCH)
+            nc.tensor.matmul_mx(
+                out=z[:],
+                lhsT=hT_codes[t][:, rows].bitcast(FP8X4),
+                lhsT_scale=hT_scales[t][:, rows],
+                rhs=w_codes["r"][:, I * D : (I + 1) * D].bitcast(FP8X4),
+                rhs_scale=w_scales["r"][:, I * D : (I + 1) * D],
+                start=True,
+                stop=True,
+            )
+            return z
 
-        def preactivation(t, g, q):
+        xz_i = const.tile([P, D], F32, name="xz_i")
+
+        def input_term():
+            z = z_psum.tile([P, D], F32, name="z")
+            nc.tensor.matmul_mx(
+                out=z[:],
+                lhsT=xT_codes[:, 0:BATCH].bitcast(FP8X4),
+                lhsT_scale=xT_scales[:, 0:BATCH],
+                rhs=w_codes["k"][:, I * D : (I + 1) * D].bitcast(FP8X4),
+                rhs_scale=w_scales["k"][:, I * D : (I + 1) * D],
+                start=True,
+                stop=True,
+            )
+            nc.vector.tensor_tensor(out=xz_i[:], in0=z[:], in1=bias_i[:], op=ADD)
+
+        def weights_stationary(t, g, q):
             cols = slice((g * BLOCKS + q) * P, (g * BLOCKS + q + 1) * P)
             z = z_psum.tile([P, MOVING], F32, name="z")
             nc.tensor.matmul_mx(
@@ -198,48 +250,79 @@ def tile_rlstmcell_pb_kernel(
             )
             return z
 
-        def sigmoid(z, g, q):
-            gateT = gate_pool.tile([P, MOVING], F32, name="gateT")
-            m = g * BLOCKS + q
-            nc.scalar.activation(
-                out=gateT[:], in_=z[:], func=SIGMOID, bias=bias_cols[:, m : m + 1], scale=1.0
-            )
-            return gateT
+        def block(tile3, q):
+            return tile3[:, :, q * P : (q + 1) * P]
 
-        def to_batch_rows(gateT):
+        cand, c_new, h_new, gate_i, tanh_c, kept = {}, {}, {}, {}, {}, {}
+
+        def tanh_candidate(t):
+            cand[t] = work.tile([P, GROUP, D], F32, name="cand", bufs=4)
+            nc.scalar.activation(out=cand[t][:], in_=cu_sb[t][:], func=TANH)
+
+        def input_preactivation(t, s):
+            gate_i[(t, s)] = gate_pool.tile([P, D], F32, name="gate_i", bufs=8)
+            nc.vector.tensor_tensor(
+                out=gate_i[(t, s)][:], in0=zs[(t, I, s)][:], in1=xz_i[:], op=ADD
+            )
+
+        def input_gate(t, s):
+            nc.scalar.activation(out=gate_i[(t, s)][:], in_=gate_i[(t, s)][:], func=SIGMOID)
+
+        def apply_input_gate(t, s):
+            nc.gpsimd.tensor_tensor(
+                out=cand[t][:, s, :], in0=gate_i[(t, s)][:], in1=cand[t][:, s, :], op=MULT
+            )
+
+        def transposed_gate(t, g, q):
+            gatesT[(t, g, q)] = gate_pool.tile([P, MOVING], F32, name="gateT", bufs=2 * BLOCKS)
+            m = (g - 1) * BLOCKS + q
+            nc.scalar.activation(
+                out=gatesT[(t, g, q)][:],
+                in_=zs[(t, g, q)][:],
+                func=SIGMOID,
+                bias=bias_cols[:, m : m + 1],
+                scale=1.0,
+            )
+
+        def to_batch_rows(t, g, q):
             gate = t_psum.tile([P, GROUP * P], F32, name="gate", tag="t")
             for s in range(GROUP):
-                nc.tensor.transpose(gate[:, s * P : (s + 1) * P], gateT[:, s * P : (s + 1) * P], ident[:])
-            return gate[:].rearrange("b (s d) -> b s d", s=GROUP)
-
-        cand, keep, c_new, tanh_c, h_new = {}, {}, {}, {}, {}
-
-        def tanh_candidate(t, first_slot, slots):
-            if first_slot == 0:
-                cand[t] = work.tile([P, GROUP, D], F32, name="cand")
-            part = slice(first_slot, first_slot + slots)
-            nc.scalar.activation(out=cand[t][:, part, :], in_=cu_sb[t][:, part, :], func=TANH)
-
-        def apply_gate(t, g, q, gate):
-            if g == 0:
-                nc.vector.tensor_tensor(out=block(cand[t], q), in0=gate, in1=block(cand[t], q), op=MULT)
-            if g == 1:
-                if q == 0:
-                    keep[t] = work.tile([P, GROUP, D], F32, name="keep")
-                    c_new[t] = work.tile([P, GROUP, D], F32, name="c_new")
-                nc.vector.tensor_tensor(out=block(keep[t], q), in0=gate, in1=block(c_sb[t], q), op=MULT)
-                nc.gpsimd.tensor_tensor(
-                    out=block(c_new[t], q), in0=block(keep[t], q), in1=block(cand[t], q), op=ADD
+                nc.tensor.transpose(
+                    gate[:, s * P : (s + 1) * P], gatesT[(t, g, q)][:, s * P : (s + 1) * P], ident[:]
                 )
-            if g == 2:
-                if q == 0:
-                    h_new[t] = work.tile([P, GROUP, D], F32, name="h_new")
-                nc.vector.tensor_tensor(out=block(h_new[t], q), in0=gate, in1=block(tanh_c[t], q), op=MULT)
+            gates[(t, g, q)] = gate[:].rearrange("b (s d) -> b s d", s=GROUP)
+
+        def apply_forget_gate(t, q):
+            if q == 0:
+                c_new[t] = work.tile([P, GROUP, D], F32, name="c_new")
+            kept[(t, q)] = block_pool.tile([P, GROUP, P], F32, name="kept")
+            nc.vector.tensor_tensor(
+                out=kept[(t, q)][:], in0=gates[(t, F, q)], in1=block(c_sb[t], q), op=MULT
+            )
+
+        def new_cell(t, q, add):
+            add(
+                out=block(c_new[t], q), in0=kept[(t, q)][:], in1=block(cand[t], q), op=ADD
+            )
 
         def tanh_cell(t, q):
+            tanh_c[(t, q)] = block_pool.tile([P, GROUP, P], F32, name="tanh_c")
+            nc.scalar.activation(out=tanh_c[(t, q)][:], in_=block(c_new[t], q), func=TANH)
+
+        def new_h(t, q):
             if q == 0:
-                tanh_c[t] = work.tile([P, GROUP, D], F32, name="tanh_c")
-            nc.scalar.activation(out=block(tanh_c[t], q), in_=block(c_new[t], q), func=TANH)
+                h_new[t] = work.tile([P, GROUP, D], F32, name="h_new")
+            nc.vector.tensor_tensor(
+                out=block(h_new[t], q), in0=gates[(t, O, q)], in1=tanh_c[(t, q)][:], op=MULT
+            )
+
+        def store_columns(out, t, tile3, cols):
+            nc.sync.dma_start(
+                out=out[:, t * GROUP * D : (t + 1) * GROUP * D].rearrange(
+                    "b (s d) -> b s d", s=GROUP
+                )[:, :, cols],
+                in_=tile3[:, :, cols],
+            )
 
         def store(out, t, tile3):
             nc.sync.dma_start(
@@ -247,45 +330,89 @@ def tile_rlstmcell_pb_kernel(
                 in_=tile3[:].rearrange("b s d -> b (s d)"),
             )
 
-        transpose_h(0, 0, nc.scalar.copy)
-        transpose_h(0, 1, nc.scalar.copy)
-        nc.vector.quantize_mx(out=xT_codes[:].bitcast(FP8X4), scales=xT_scales[:], in_=xT_grouped[:])
-        regroup_weights(0)
-        quantise_h(0)
-        quantise_weights(0)
+        zs, gatesT, gates = {}, {}, {}
 
-        rounds = [(t, g) for t in range(GROUPS) for g in range(GATES)]
-        gatesT = {}
-        for r in range(len(rounds) + 1):
-            if r < len(rounds):
-                t, g = rounds[r]
-                zs = [preactivation(t, g, q) for q in range(BLOCKS)]
-                if t == 0 and g + 1 < GATES:
-                    regroup_weights(g + 1)
-                    quantise_weights(g + 1)
+        vcopy, scopy = nc.vector.tensor_copy, nc.scalar.copy
+        transpose_x()
+        transpose_h(0, 0, scopy)
+        transpose_h(0, 1, scopy)
+        spread_biases()
+        regroup_weights("r", F, vcopy)
+        for s in range(GROUP):
+            quantise_x(s)
+        quantise_weights("r", F)
+        quantise_h(0)
+        regroup_weights("k", F, vcopy)
+        quantise_weights("k", F)
+        for q in range(BLOCKS):
+            zs[(0, F, q)] = weights_stationary(0, F, q)
+        tanh_candidate(0)
+        for q in range(BLOCKS):
+            transposed_gate(0, F, q)
+        transpose_h(1, 0, scopy)
+        transpose_h(1, 1, scopy)
+        regroup_weights("r", I, vcopy)
+        regroup_weights("k", I, vcopy)
+        quantise_weights("r", I)
+        quantise_weights("k", I)
+        tanh_candidate(1)
+        input_term()
+        for s in range(GROUP):
+            zs[(0, I, s)] = h_stationary(0, s)
+            input_preactivation(0, s)
+        for s in range(GROUP):
+            input_gate(0, s)
+            apply_input_gate(0, s)
+        regroup_weights("r", O, vcopy)
+        regroup_weights("k", O, vcopy)
+        quantise_weights("r", O)
+        quantise_weights("k", O)
+        tanh_candidate(2)
+        tanh_candidate(3)
+
+        for t in range(GROUPS):
+            last = t + 1 == GROUPS
+            for q in range(BLOCKS):
+                zs[(t, O, q)] = weights_stationary(t, O, q)
+                transposed_gate(t, O, q)
+            if t == 0:
+                quantise_h(1)
+                for s in range(GROUP):
+                    zs[(1, I, s)] = h_stationary(1, s)
+                    input_preactivation(1, s)
+                for s in range(GROUP):
+                    input_gate(1, s)
+                    apply_input_gate(1, s)
+            add = nc.gpsimd.tensor_tensor if t < 2 else nc.vector.tensor_tensor
+            for q in range(BLOCKS):
+                to_batch_rows(t, F, q)
+                apply_forget_gate(t, q)
+                if q > 0:
+                    new_cell(t, q - 1, add)
+            new_cell(t, BLOCKS - 1, add)
+            store(out_1, t, c_new[t])
+            if t + 2 < GROUPS:
+                transpose_h(t + 2, 0, vcopy)
+                transpose_h(t + 2, 1, vcopy)
+            if not last:
                 for q in range(BLOCKS):
-                    gatesT[(r, q)] = sigmoid(zs[q], g, q)
-                    if g == 0 and t > 0:
-                        tanh_cell(t - 1, q)
-                if r == 0:
-                    tanh_candidate(0, 0, GROUP)
-                if g > 0 and t + 1 < GROUPS:
-                    tanh_candidate(t + 1, (g - 1) * 2, 2)
-            else:
-                for q in range(BLOCKS):
-                    tanh_cell(GROUPS - 1, q)
-            if r > 0:
-                t_done, g_done = rounds[r - 1]
-                for q in range(BLOCKS):
-                    apply_gate(t_done, g_done, q, to_batch_rows(gatesT[(r - 1, q)]))
-                if g_done == 1:
-                    store(out_1, t_done, c_new[t_done])
-                if g_done == 2:
-                    store(out_0, t_done, h_new[t_done])
-            if r < len(rounds):
-                t, g = rounds[r]
-                if t + 1 < GROUPS:
-                    if g < 2:
-                        transpose_h(t + 1, g, nc.vector.tensor_copy)
-                    else:
-                        quantise_h(t + 1)
+                    zs[(t + 1, F, q)] = weights_stationary(t + 1, F, q)
+                    transposed_gate(t + 1, F, q)
+            for q in range(BLOCKS):
+                to_batch_rows(t, O, q)
+            if t + 2 < GROUPS:
+                quantise_h(t + 2)
+                for s in range(GROUP):
+                    zs[(t + 2, I, s)] = h_stationary(t + 2, s)
+                    input_preactivation(t + 2, s)
+            for q in range(BLOCKS):
+                tanh_cell(t, q)
+                new_h(t, q)
+                if last and q % 2 == 1:
+                    store_columns(out_0, t, h_new[t], slice((q - 1) * P, (q + 1) * P))
+            if not last:
+                store(out_0, t, h_new[t])
+            if t + 2 < GROUPS:
+                for s in range(GROUP):
+                    input_gate(t + 2, s)
+                    apply_input_gate(t + 2, s)

@@ -41,8 +41,8 @@ def tile_rlstmcell_pb_kernel(
         gate_pool = ctx.enter_context(tc.tile_pool(name="gate_pool", bufs=2 * BLOCKS))
         block_pool = ctx.enter_context(tc.tile_pool(name="block_pool", bufs=BLOCKS))
         work = ctx.enter_context(tc.tile_pool(name="work", bufs=2))
-        z_psum = ctx.enter_context(tc.psum_pool(name="z_psum", bufs=4))
-        t_psum = ctx.enter_context(tc.psum_pool(name="t_psum", bufs=4))
+        z_psum = ctx.enter_context(tc.psum_pool(name="z_psum", bufs=5))
+        t_psum = ctx.enter_context(tc.psum_pool(name="t_psum", bufs=3))
         ctx.enter_context(tc.manual_schedule())
 
         weights = {"r": recurrent_kernel, "k": kernel}
@@ -73,23 +73,24 @@ def tile_rlstmcell_pb_kernel(
             )
 
         bias_rows = const.tile([P, P], BF16, name="bias_rows")
-        nc.vector.memset(bias_rows[:], 0.0)
+        nc.gpsimd.memset(bias_rows[:], 0.0)
         bias_row = const.tile([P, D], BF16, name="bias_row")
-        nc.vector.memset(bias_row[:], 0.0)
+        nc.gpsimd.memset(bias_row[:], 0.0)
         ones = const.tile([P, P], BF16, name="ones")
-        nc.vector.memset(ones[:], 1.0)
-        nc.sync.dma_start(
-            out=bias_rows[0 : (GATES - 1) * BLOCKS, :],
-            in_=bias[D : GATES * D].rearrange("(m p) -> m p", p=P),
-        )
-        nc.sync.dma_start(
-            out=bias_row[0:1, :], in_=bias[0:D].rearrange("(m p) -> m p", p=D)
-        )
+        nc.gpsimd.memset(ones[:], 1.0)
+
+        def load_biases():
+            nc.sync.dma_start(
+                out=bias_rows[0 : (GATES - 1) * BLOCKS, :],
+                in_=bias[D : GATES * D].rearrange("(m p) -> m p", p=P),
+            )
+            nc.sync.dma_start(out=bias_row[0:1, :], in_=bias[0:D].rearrange("(m p) -> m p", p=D))
 
         load_weights("r", F)
         x_sb = resident.tile([P, D], BF16, name="x_sb")
         nc.sync.dma_start(out=x_sb[:], in_=inputs)
         load_h(0)
+        load_biases()
         load_weights("k", F)
         load_candidate(0)
         load_h(1)
@@ -113,6 +114,8 @@ def tile_rlstmcell_pb_kernel(
 
         ident = const.tile([P, P], F32, name="ident")
         make_identity(nc, ident[:])
+        ident_bf16 = const.tile([P, P], BF16, name="ident_bf16")
+        nc.gpsimd.tensor_copy(out=ident_bf16[:], in_=ident[:])
 
         xT_codes = resident.tile([P, MOVING], U32, name="xT_codes", align_bytes=64)
         xT_scales = resident.tile([P, MOVING], U8, name="xT_scales", align_bytes=64)
@@ -140,10 +143,10 @@ def tile_rlstmcell_pb_kernel(
         bias_i = const.tile([P, D], F32, name="bias_i")
 
         def spread_biases():
-            bias_rows_f32 = const.tile([P, P], F32, name="bias_rows_f32")
-            nc.vector.tensor_copy(out=bias_rows_f32[:], in_=bias_rows[:])
             bias_ps = t_psum.tile([P, MOVING], F32, name="bias_ps", tag="t")
-            nc.tensor.transpose(bias_ps[:, 0:P], bias_rows_f32[:], ident[:])
+            nc.tensor.matmul(
+                bias_ps[:, 0:P], lhsT=bias_rows[:], rhs=ident_bf16[:], start=True, stop=True
+            )
             nc.scalar.copy(out=bias_cols[:], in_=bias_ps[:, 0 : (GATES - 1) * BLOCKS])
             spread = t_psum.tile([P, D], F32, name="spread", tag="t")
             nc.tensor.matmul(spread[:], lhsT=ones[:], rhs=bias_row[:], start=True, stop=True)
@@ -255,9 +258,11 @@ def tile_rlstmcell_pb_kernel(
 
         cand, c_new, h_new, gate_i, tanh_c, kept = {}, {}, {}, {}, {}, {}
 
-        def tanh_candidate(t):
-            cand[t] = work.tile([P, GROUP, D], F32, name="cand", bufs=4)
-            nc.scalar.activation(out=cand[t][:], in_=cu_sb[t][:], func=TANH)
+        def tanh_candidate(t, first=0, count=GROUP):
+            if first == 0:
+                cand[t] = work.tile([P, GROUP, D], F32, name="cand", bufs=4)
+            part = slice(first, first + count)
+            nc.scalar.activation(out=cand[t][:, part, :], in_=cu_sb[t][:, part, :], func=TANH)
 
         def input_preactivation(t, s):
             gate_i[(t, s)] = gate_pool.tile([P, D], F32, name="gate_i", bufs=8)
@@ -355,6 +360,7 @@ def tile_rlstmcell_pb_kernel(
         regroup_weights("k", I, vcopy)
         quantise_weights("r", I)
         quantise_weights("k", I)
+        quantise_h(1)
         tanh_candidate(1)
         input_term()
         for s in range(GROUP):
@@ -369,50 +375,67 @@ def tile_rlstmcell_pb_kernel(
         quantise_weights("k", O)
         tanh_candidate(2)
         tanh_candidate(3)
+        zs[(0, O, 0)] = weights_stationary(0, O, 0)
+        zs[(1, F, 0)] = weights_stationary(1, F, 0)
+        for s in range(2):
+            zs[(1, I, s)] = h_stationary(1, s)
+        to_batch_rows(0, F, 0)
+        apply_forget_gate(0, 0)
+        for s in range(2):
+            input_preactivation(1, s)
+        new_cell(0, 0, nc.gpsimd.tensor_tensor)
 
-        for t in range(GROUPS):
-            last = t + 1 == GROUPS
-            for q in range(BLOCKS):
-                zs[(t, O, q)] = weights_stationary(t, O, q)
-                transposed_gate(t, O, q)
-            if t == 0:
-                quantise_h(1)
-                for s in range(GROUP):
-                    zs[(1, I, s)] = h_stationary(1, s)
-                    input_preactivation(1, s)
-                for s in range(GROUP):
-                    input_gate(1, s)
-                    apply_input_gate(1, s)
-            add = nc.gpsimd.tensor_tensor if t < 2 else nc.vector.tensor_tensor
-            for q in range(BLOCKS):
-                to_batch_rows(t, F, q)
-                apply_forget_gate(t, q)
-                if q > 0:
-                    new_cell(t, q - 1, add)
-            new_cell(t, BLOCKS - 1, add)
-            store(out_1, t, c_new[t])
-            if t + 2 < GROUPS:
-                transpose_h(t + 2, 0, vcopy)
-                transpose_h(t + 2, 1, vcopy)
-            if not last:
-                for q in range(BLOCKS):
-                    zs[(t + 1, F, q)] = weights_stationary(t + 1, F, q)
-                    transposed_gate(t + 1, F, q)
-            for q in range(BLOCKS):
-                to_batch_rows(t, O, q)
-            if t + 2 < GROUPS:
-                quantise_h(t + 2)
-                for s in range(GROUP):
-                    zs[(t + 2, I, s)] = h_stationary(t + 2, s)
-                    input_preactivation(t + 2, s)
-            for q in range(BLOCKS):
-                tanh_cell(t, q)
+
+        steps = SLOTS
+        for j in range(steps + 1):
+            o, f, i = j + 1, j + 5, j + 6
+            if o < steps:
+                zs[(o // 4, O, o % 4)] = weights_stationary(o // 4, O, o % 4)
+            if f < steps:
+                zs[(f // 4, F, f % 4)] = weights_stationary(f // 4, F, f % 4)
+            if i < steps:
+                zs[(i // 4, I, i % 4)] = h_stationary(i // 4, i % 4)
+            if j < steps:
+                transposed_gate(j // 4, O, j % 4)
+            if f - 1 < steps:
+                transposed_gate((f - 1) // 4, F, (f - 1) % 4)
+            if j == 0:
+                input_gate(1, 0)
+            if i - 1 < steps:
+                input_gate((i - 1) // 4, (i - 1) % 4)
+            if j < steps:
+                tanh_cell(j // 4, j % 4)
+            for t in (2, 3):
+                if j == 4 * t - 8:
+                    transpose_h(t, 0, vcopy)
+                if j == 4 * t - 7:
+                    transpose_h(t, 1, vcopy)
+            if o < steps:
+                to_batch_rows(o // 4, F, o % 4)
+            if j > 0:
+                to_batch_rows((j - 1) // 4, O, (j - 1) % 4)
+            if i < steps:
+                input_preactivation(i // 4, i % 4)
+            if o < steps:
+                apply_forget_gate(o // 4, o % 4)
+            for t in (2, 3):
+                if j == 4 * t - 7:
+                    quantise_h(t)
+            if j > 0:
+                t, q = (j - 1) // 4, (j - 1) % 4
                 new_h(t, q)
-                if last and q % 2 == 1:
-                    store_columns(out_0, t, h_new[t], slice((q - 1) * P, (q + 1) * P))
-            if not last:
-                store(out_0, t, h_new[t])
-            if t + 2 < GROUPS:
-                for s in range(GROUP):
-                    input_gate(t + 2, s)
-                    apply_input_gate(t + 2, s)
+                if t == GROUPS - 1:
+                    store_columns(out_0, t, h_new[t], slice(q * P, (q + 1) * P))
+                elif q == BLOCKS - 1:
+                    store(out_0, t, h_new[t])
+            if o < steps:
+                new_cell(o // 4, o % 4, nc.vector.tensor_tensor if (o % 4 == 3 and o < 12) or o == 15 else nc.gpsimd.tensor_tensor)
+                if o >= steps - 4:
+                    if o % 2 == 1:
+                        store_columns(out_1, o // 4, c_new[o // 4], slice((o % 4 - 1) * P, (o % 4 + 1) * P))
+                elif o % 4 == 3:
+                    store(out_1, o // 4, c_new[o // 4])
+            if j == 0:
+                apply_input_gate(1, 0)
+            if i - 1 < steps:
+                apply_input_gate((i - 1) // 4, (i - 1) % 4)

@@ -429,7 +429,7 @@ def tile_rlstmcell_pb_kernel(
                 elif q == BLOCKS - 1:
                     store(out_0, t, h_new[t])
             if o < steps:
-                new_cell(o // 4, o % 4, nc.vector.tensor_tensor if (o % 4 == 3 and o < 12) or o == 15 else nc.gpsimd.tensor_tensor)
+                new_cell(o // 4, o % 4, nc.vector.tensor_tensor)
                 if o >= steps - 4:
                     if o % 2 == 1:
                         store_columns(out_1, o // 4, c_new[o // 4], slice((o % 4 - 1) * P, (o % 4 + 1) * P))

@@ -56,7 +56,7 @@ def tile_rlstmcell_pb_kernel(
             )
 
         def load_h(t):
-            h_sb[t] = loads.tile([P, GROUP * D], BF16, name="h_rows")
+            h_sb[t] = loads.tile([P, GROUP * D], BF16, name="h_rows", bufs=GROUPS)
             nc.sync.dma_start(out=h_sb[t][:], in_=h_state[:, t * GROUP * D : (t + 1) * GROUP * D])
 
         def load_candidate(t):
@@ -81,8 +81,7 @@ def tile_rlstmcell_pb_kernel(
 
         def load_biases():
             nc.sync.dma_start(
-                out=bias_rows[0 : (GATES - 1) * BLOCKS, :],
-                in_=bias[D : GATES * D].rearrange("(m p) -> m p", p=P),
+                out=bias_rows[0 : GATES * BLOCKS, :], in_=bias.rearrange("(m p) -> m p", p=P)
             )
             nc.sync.dma_start(out=bias_row[0:1, :], in_=bias[0:D].rearrange("(m p) -> m p", p=D))
 
@@ -96,15 +95,15 @@ def tile_rlstmcell_pb_kernel(
         load_h(1)
         load_weights("r", I)
         load_weights("k", I)
-        load_candidate(1)
-        load_cell(0)
+        load_h(2)
         load_weights("r", O)
         load_weights("k", O)
+        load_h(3)
+        load_candidate(1)
+        load_cell(0)
         load_candidate(2)
-        load_h(2)
         load_cell(1)
         load_candidate(3)
-        load_h(3)
         load_cell(2)
         load_cell(3)
 
@@ -139,15 +138,17 @@ def tile_rlstmcell_pb_kernel(
                 out=xT_codes[:, cols].bitcast(FP8X4), scales=xT_scales[:, cols], in_=xT_grouped[:]
             )
 
-        bias_cols = const.tile([P, (GATES - 1) * BLOCKS], F32, name="bias_cols")
+        bias_cols = const.tile([P, GATES * BLOCKS], F32, name="bias_cols")
         bias_i = const.tile([P, D], F32, name="bias_i")
 
-        def spread_biases():
+        def biases_to_columns():
             bias_ps = t_psum.tile([P, MOVING], F32, name="bias_ps", tag="t")
             nc.tensor.matmul(
                 bias_ps[:, 0:P], lhsT=bias_rows[:], rhs=ident_bf16[:], start=True, stop=True
             )
-            nc.scalar.copy(out=bias_cols[:], in_=bias_ps[:, 0 : (GATES - 1) * BLOCKS])
+            nc.scalar.copy(out=bias_cols[:], in_=bias_ps[:, 0 : GATES * BLOCKS])
+
+        def spread_input_bias():
             spread = t_psum.tile([P, D], F32, name="spread", tag="t")
             nc.tensor.matmul(spread[:], lhsT=ones[:], rhs=bias_row[:], start=True, stop=True)
             nc.scalar.copy(out=bias_i[:], in_=spread[:])
@@ -177,8 +178,8 @@ def tile_rlstmcell_pb_kernel(
             )
 
         def quantise_h(t):
-            hT_codes[t] = stage.tile([P, MOVING], U32, name="hT_codes", align_bytes=64)
-            hT_scales[t] = stage.tile([P, MOVING], U8, name="hT_scales", align_bytes=64)
+            hT_codes[t] = stage.tile([P, MOVING], U32, name="hT_codes", bufs=GROUPS, align_bytes=64)
+            hT_scales[t] = stage.tile([P, MOVING], U8, name="hT_scales", bufs=GROUPS, align_bytes=64)
             nc.vector.quantize_mx(
                 out=hT_codes[t][:].bitcast(FP8X4), scales=hT_scales[t][:], in_=hT_grouped[t][:]
             )
@@ -228,6 +229,9 @@ def tile_rlstmcell_pb_kernel(
                 start=True,
                 stop=True,
             )
+            return z
+
+        def add_input_bias(z):
             nc.vector.tensor_tensor(out=xz_i[:], in0=z[:], in1=bias_i[:], op=ADD)
 
         def weights_stationary(t, g, q):
@@ -265,7 +269,7 @@ def tile_rlstmcell_pb_kernel(
             nc.scalar.activation(out=cand[t][:, part, :], in_=cu_sb[t][:, part, :], func=TANH)
 
         def input_preactivation(t, s):
-            gate_i[(t, s)] = gate_pool.tile([P, D], F32, name="gate_i", bufs=8)
+            gate_i[(t, s)] = gate_pool.tile([P, D], F32, name="gate_i", bufs=6)
             nc.vector.tensor_tensor(
                 out=gate_i[(t, s)][:], in0=zs[(t, I, s)][:], in1=xz_i[:], op=ADD
             )
@@ -278,9 +282,14 @@ def tile_rlstmcell_pb_kernel(
                 out=cand[t][:, s, :], in0=gate_i[(t, s)][:], in1=cand[t][:, s, :], op=MULT
             )
 
+        def apply_transposed_input_gate(t, q):
+            nc.vector.tensor_tensor(
+                out=block(cand[t], q), in0=gates[(t, I, q)], in1=block(cand[t], q), op=MULT
+            )
+
         def transposed_gate(t, g, q):
-            gatesT[(t, g, q)] = gate_pool.tile([P, MOVING], F32, name="gateT", bufs=2 * BLOCKS)
-            m = (g - 1) * BLOCKS + q
+            gatesT[(t, g, q)] = gate_pool.tile([P, MOVING], F32, name="gateT", bufs=3 * BLOCKS)
+            m = g * BLOCKS + q
             nc.scalar.activation(
                 out=gatesT[(t, g, q)][:],
                 in_=zs[(t, g, q)][:],
@@ -341,7 +350,8 @@ def tile_rlstmcell_pb_kernel(
         transpose_x()
         transpose_h(0, 0, scopy)
         transpose_h(0, 1, scopy)
-        spread_biases()
+        biases_to_columns()
+        spread_input_bias()
         regroup_weights("r", F, vcopy)
         for s in range(GROUP):
             quantise_x(s)
@@ -361,30 +371,33 @@ def tile_rlstmcell_pb_kernel(
         quantise_weights("r", I)
         quantise_weights("k", I)
         quantise_h(1)
-        tanh_candidate(1)
-        input_term()
-        for s in range(GROUP):
-            zs[(0, I, s)] = h_stationary(0, s)
-            input_preactivation(0, s)
-        for s in range(GROUP):
-            input_gate(0, s)
-            apply_input_gate(0, s)
+        transpose_h(2, 0, scopy)
+        transpose_h(2, 1, scopy)
+        xz = input_term()
+        for q in range(BLOCKS):
+            zs[(0, I, q)] = weights_stationary(0, I, q)
+        for q in range(BLOCKS):
+            transposed_gate(0, I, q)
         regroup_weights("r", O, vcopy)
+        add_input_bias(xz)
+        transpose_h(3, 0, scopy)
+        transpose_h(3, 1, scopy)
         regroup_weights("k", O, vcopy)
         quantise_weights("r", O)
         quantise_weights("k", O)
-        tanh_candidate(2)
-        tanh_candidate(3)
+        quantise_h(2)
         zs[(0, O, 0)] = weights_stationary(0, O, 0)
         zs[(1, F, 0)] = weights_stationary(1, F, 0)
         for s in range(2):
             zs[(1, I, s)] = h_stationary(1, s)
+            input_preactivation(1, s)
+        for q in range(BLOCKS):
+            to_batch_rows(0, I, q)
+            apply_transposed_input_gate(0, q)
+        quantise_h(3)
         to_batch_rows(0, F, 0)
         apply_forget_gate(0, 0)
-        for s in range(2):
-            input_preactivation(1, s)
         new_cell(0, 0, nc.gpsimd.tensor_tensor)
-
 
         steps = SLOTS
         for j in range(steps + 1):
@@ -400,16 +413,14 @@ def tile_rlstmcell_pb_kernel(
             if f - 1 < steps:
                 transposed_gate((f - 1) // 4, F, (f - 1) % 4)
             if j == 0:
+                tanh_candidate(1)
                 input_gate(1, 0)
             if i - 1 < steps:
                 input_gate((i - 1) // 4, (i - 1) % 4)
             if j < steps:
                 tanh_cell(j // 4, j % 4)
-            for t in (2, 3):
-                if j == 4 * t - 8:
-                    transpose_h(t, 0, vcopy)
-                if j == 4 * t - 7:
-                    transpose_h(t, 1, vcopy)
+            if j in (1, 5):
+                tanh_candidate(2 + j // 5)
             if o < steps:
                 to_batch_rows(o // 4, F, o % 4)
             if j > 0:
@@ -418,9 +429,6 @@ def tile_rlstmcell_pb_kernel(
                 input_preactivation(i // 4, i % 4)
             if o < steps:
                 apply_forget_gate(o // 4, o % 4)
-            for t in (2, 3):
-                if j == 4 * t - 7:
-                    quantise_h(t)
             if j > 0:
                 t, q = (j - 1) // 4, (j - 1) % 4
                 new_h(t, q)
@@ -429,7 +437,7 @@ def tile_rlstmcell_pb_kernel(
                 elif q == BLOCKS - 1:
                     store(out_0, t, h_new[t])
             if o < steps:
-                new_cell(o // 4, o % 4, nc.vector.tensor_tensor)
+                new_cell(o // 4, o % 4, nc.vector.tensor_tensor if o == 15 else nc.gpsimd.tensor_tensor)
                 if o >= steps - 4:
                     if o % 2 == 1:
                         store_columns(out_1, o // 4, c_new[o // 4], slice((o % 4 - 1) * P, (o % 4 + 1) * P))

@@ -56,7 +56,7 @@ def tile_rlstmcell_pb_kernel(
             )
 
         def load_h(t):
-            h_sb[t] = loads.tile([P, GROUP * D], BF16, name="h_rows", bufs=GROUPS)
+            h_sb[t] = loads.tile([P, GROUP * D], BF16, name="h_rows", bufs=3)
             nc.sync.dma_start(out=h_sb[t][:], in_=h_state[:, t * GROUP * D : (t + 1) * GROUP * D])
 
         def load_candidate(t):
@@ -189,7 +189,7 @@ def tile_rlstmcell_pb_kernel(
         w_scales = {w: resident.tile([P, GATES * D], U8, name="scales_" + w, align_bytes=64) for w in weights}
 
         def regroup_weights(w, g, copy):
-            w_grouped[w] = stage.tile([P, D, PACK], BF16, name="grouped_" + w, align_bytes=64)
+            w_grouped[w] = stage.tile([P, D, PACK], BF16, name="grouped_" + w, bufs=1, align_bytes=64)
             copy(
                 out=w_grouped[w][:].rearrange("p (c i) t -> p c t i", i=4),
                 in_=w_raw[(w, g)][:].rearrange("p t (c i) -> p c t i", i=4),
@@ -269,18 +269,19 @@ def tile_rlstmcell_pb_kernel(
             nc.scalar.activation(out=cand[t][:, part, :], in_=cu_sb[t][:, part, :], func=TANH)
 
         def input_preactivation(t, s):
-            gate_i[(t, s)] = gate_pool.tile([P, D], F32, name="gate_i", bufs=6)
+            if s % 2 == 0:
+                gate_i[(t, s // 2)] = gate_pool.tile([P, 2, D], F32, name="gate_i", bufs=3)
             nc.vector.tensor_tensor(
-                out=gate_i[(t, s)][:], in0=zs[(t, I, s)][:], in1=xz_i[:], op=ADD
+                out=gate_i[(t, s // 2)][:, s % 2, :], in0=zs[(t, I, s)][:], in1=xz_i[:], op=ADD
             )
 
         def input_gate(t, s):
-            nc.scalar.activation(out=gate_i[(t, s)][:], in_=gate_i[(t, s)][:], func=SIGMOID)
+            gate = gate_i[(t, s // 2)][:, s % 2, :]
+            nc.scalar.activation(out=gate, in_=gate, func=SIGMOID)
 
-        def apply_input_gate(t, s):
-            nc.gpsimd.tensor_tensor(
-                out=cand[t][:, s, :], in0=gate_i[(t, s)][:], in1=cand[t][:, s, :], op=MULT
-            )
+        def apply_input_gate(t, pair):
+            part = cand[t][:, 2 * pair : 2 * pair + 2, :]
+            nc.gpsimd.tensor_tensor(out=part, in0=gate_i[(t, pair)][:], in1=part, op=MULT)
 
         def apply_transposed_input_gate(t, q):
             nc.vector.tensor_tensor(
@@ -308,15 +309,20 @@ def tile_rlstmcell_pb_kernel(
 
         def apply_forget_gate(t, q):
             if q == 0:
-                c_new[t] = work.tile([P, GROUP, D], F32, name="c_new")
-            kept[(t, q)] = block_pool.tile([P, GROUP, P], F32, name="kept")
+                c_new[t] = work.tile([P, GROUP, D], F32, name="c_new", bufs=3)
+            if q % 2 == 0:
+                kept[(t, q // 2)] = block_pool.tile([P, GROUP, 2 * P], F32, name="kept", bufs=3)
             nc.vector.tensor_tensor(
-                out=kept[(t, q)][:], in0=gates[(t, F, q)], in1=block(c_sb[t], q), op=MULT
+                out=block(kept[(t, q // 2)], q % 2),
+                in0=gates[(t, F, q)],
+                in1=block(c_sb[t], q),
+                op=MULT,
             )
 
-        def new_cell(t, q, add):
-            add(
-                out=block(c_new[t], q), in0=kept[(t, q)][:], in1=block(cand[t], q), op=ADD
+        def new_cell(t, pair):
+            cols = slice(2 * pair * P, (2 * pair + 2) * P)
+            nc.gpsimd.tensor_tensor(
+                out=c_new[t][:, :, cols], in0=kept[(t, pair)][:], in1=cand[t][:, :, cols], op=ADD
             )
 
         def tanh_cell(t, q):
@@ -386,22 +392,37 @@ def tile_rlstmcell_pb_kernel(
         quantise_weights("r", O)
         quantise_weights("k", O)
         quantise_h(2)
-        zs[(0, O, 0)] = weights_stationary(0, O, 0)
-        zs[(1, F, 0)] = weights_stationary(1, F, 0)
-        for s in range(2):
-            zs[(1, I, s)] = h_stationary(1, s)
-            input_preactivation(1, s)
+        quantise_h(3)
+        for q in range(BLOCKS):
+            zs[(1, F, q)] = weights_stationary(1, F, q)
+            transposed_gate(1, F, q)
         for q in range(BLOCKS):
             to_batch_rows(0, I, q)
             apply_transposed_input_gate(0, q)
-        quantise_h(3)
-        to_batch_rows(0, F, 0)
-        apply_forget_gate(0, 0)
-        new_cell(0, 0, nc.gpsimd.tensor_tensor)
+        tanh_candidate(1)
+        for q in range(BLOCKS):
+            to_batch_rows(0, F, q)
+            apply_forget_gate(0, q)
+            if q % 2 == 1:
+                new_cell(0, q // 2)
+        for s in range(GROUP):
+            zs[(1, I, s)] = h_stationary(1, s)
+            input_preactivation(1, s)
+        tanh_candidate(2)
+        for s in range(GROUP):
+            input_gate(1, s)
+            if s % 2 == 1:
+                apply_input_gate(1, s // 2)
+        zs[(0, O, 0)] = weights_stationary(0, O, 0)
+        zs[(2, F, 0)] = weights_stationary(2, F, 0)
+        zs[(2, I, 0)] = h_stationary(2, 0)
+        to_batch_rows(1, F, 0)
+        input_preactivation(2, 0)
+        apply_forget_gate(1, 0)
 
         steps = SLOTS
         for j in range(steps + 1):
-            o, f, i = j + 1, j + 5, j + 6
+            o, f, i, c = j + 1, j + 9, j + 9, j + 5
             if o < steps:
                 zs[(o // 4, O, o % 4)] = weights_stationary(o // 4, O, o % 4)
             if f < steps:
@@ -412,38 +433,34 @@ def tile_rlstmcell_pb_kernel(
                 transposed_gate(j // 4, O, j % 4)
             if f - 1 < steps:
                 transposed_gate((f - 1) // 4, F, (f - 1) % 4)
-            if j == 0:
-                tanh_candidate(1)
-                input_gate(1, 0)
             if i - 1 < steps:
                 input_gate((i - 1) // 4, (i - 1) % 4)
             if j < steps:
                 tanh_cell(j // 4, j % 4)
-            if j in (1, 5):
-                tanh_candidate(2 + j // 5)
-            if o < steps:
-                to_batch_rows(o // 4, F, o % 4)
+            if j == 2:
+                tanh_candidate(3)
+            if c < steps:
+                to_batch_rows(c // 4, F, c % 4)
             if j > 0:
                 to_batch_rows((j - 1) // 4, O, (j - 1) % 4)
             if i < steps:
                 input_preactivation(i // 4, i % 4)
-            if o < steps:
-                apply_forget_gate(o // 4, o % 4)
+            if c < steps:
+                apply_forget_gate(c // 4, c % 4)
             if j > 0:
                 t, q = (j - 1) // 4, (j - 1) % 4
                 new_h(t, q)
+                if q == 1 and t < GROUPS - 1:
+                    store(out_1, t, c_new[t])
                 if t == GROUPS - 1:
                     store_columns(out_0, t, h_new[t], slice(q * P, (q + 1) * P))
+                    if q % 2 == 0:
+                        store_columns(out_1, t, c_new[t], slice(q * P, (q + 2) * P))
                 elif q == BLOCKS - 1:
                     store(out_0, t, h_new[t])
-            if o < steps:
-                new_cell(o // 4, o % 4, nc.vector.tensor_tensor if o == 15 else nc.gpsimd.tensor_tensor)
-                if o >= steps - 4:
-                    if o % 2 == 1:
-                        store_columns(out_1, o // 4, c_new[o // 4], slice((o % 4 - 1) * P, (o % 4 + 1) * P))
-                elif o % 4 == 3:
-                    store(out_1, o // 4, c_new[o // 4])
-            if j == 0:
-                apply_input_gate(1, 0)
-            if i - 1 < steps:
-                apply_input_gate((i - 1) // 4, (i - 1) % 4)
+            if c - 1 < steps:
+                t, q = (c - 1) // 4, (c - 1) % 4
+                if q % 2 == 1:
+                    new_cell(t, q // 2)
+            if i - 1 < steps and i % 2 == 0:
+                apply_input_gate((i - 1) // 4, (i - 1) % 4 // 2)

@@ -344,6 +344,9 @@ def tile_rlstmcell_pb_kernel(
                 in_=tile3[:, :, cols],
             )
 
+        def store_pair(out, t, pair, tile3):
+            store_columns(out, t, tile3, slice(2 * pair * P, (2 * pair + 2) * P))
+
         def store(out, t, tile3):
             nc.sync.dma_start(
                 out=out[:, t * GROUP * D : (t + 1) * GROUP * D],
@@ -419,6 +422,7 @@ def tile_rlstmcell_pb_kernel(
         to_batch_rows(1, F, 0)
         input_preactivation(2, 0)
         apply_forget_gate(1, 0)
+        store_pair(out_1, 0, 0, c_new[0])
 
         steps = SLOTS
         for j in range(steps + 1):
@@ -450,14 +454,14 @@ def tile_rlstmcell_pb_kernel(
             if j > 0:
                 t, q = (j - 1) // 4, (j - 1) % 4
                 new_h(t, q)
-                if q == 1 and t < GROUPS - 1:
-                    store(out_1, t, c_new[t])
-                if t == GROUPS - 1:
+                if q % 2 == 1:
+                    n = j - 1 + 2 * 1
+                    if n < steps:
+                        store_pair(out_1, n // 4, n % 4 // 2, c_new[n // 4])
+                if q % 2 == 1 and j < steps - 1:
+                    store_pair(out_0, t, q // 2, h_new[t])
+                if j > steps - 2:
                     store_columns(out_0, t, h_new[t], slice(q * P, (q + 1) * P))
-                    if q % 2 == 0:
-                        store_columns(out_1, t, c_new[t], slice(q * P, (q + 2) * P))
-                elif q == BLOCKS - 1:
-                    store(out_0, t, h_new[t])
             if c - 1 < steps:
                 t, q = (c - 1) // 4, (c - 1) % 4
                 if q % 2 == 1:

@@ -389,13 +389,10 @@ def tile_rlstmcell_pb_kernel(
             transposed_gate(0, I, q)
         regroup_weights("r", O, vcopy)
         add_input_bias(xz)
-        transpose_h(3, 0, scopy)
-        transpose_h(3, 1, scopy)
         regroup_weights("k", O, vcopy)
         quantise_weights("r", O)
         quantise_weights("k", O)
         quantise_h(2)
-        quantise_h(3)
         for q in range(BLOCKS):
             zs[(1, F, q)] = weights_stationary(1, F, q)
             transposed_gate(1, F, q)
@@ -443,12 +440,18 @@ def tile_rlstmcell_pb_kernel(
                 tanh_cell(j // 4, j % 4)
             if j == 2:
                 tanh_candidate(3)
+            if j == 0:
+                transpose_h(3, 0, vcopy)
+            if j == 1:
+                transpose_h(3, 1, vcopy)
             if c < steps:
                 to_batch_rows(c // 4, F, c % 4)
             if j > 0:
                 to_batch_rows((j - 1) // 4, O, (j - 1) % 4)
             if i < steps:
                 input_preactivation(i // 4, i % 4)
+            if j == 1:
+                quantise_h(3)
             if c < steps:
                 apply_forget_gate(c // 4, c % 4)
             if j > 0:

@@ -59,9 +59,13 @@ def tile_rlstmcell_pb_kernel(
             h_sb[t] = loads.tile([P, GROUP * D], BF16, name="h_rows", bufs=3)
             nc.sync.dma_start(out=h_sb[t][:], in_=h_state[:, t * GROUP * D : (t + 1) * GROUP * D])
 
-        def load_candidate(t):
-            cu_sb[t] = loads.tile([P, GROUP, D], BF16, name="candidate_rows")
-            nc.sync.dma_start(out=cu_sb[t][:], in_=c_upd[:, t * GROUP : (t + 1) * GROUP, :])
+        def load_candidate(t, first=0, count=GROUP):
+            if first == 0:
+                cu_sb[t] = loads.tile([P, GROUP, D], BF16, name="candidate_rows")
+            slot = t * GROUP + first
+            nc.sync.dma_start(
+                out=cu_sb[t][:, first : first + count, :], in_=c_upd[:, slot : slot + count, :]
+            )
 
         def load_cell(t):
             c_sb[t] = loads.tile([P, GROUP, D], BF16, name="cell_rows")
@@ -365,21 +369,20 @@ def tile_rlstmcell_pb_kernel(
         for s in range(GROUP):
             quantise_x(s)
         quantise_weights("r", F)
-        quantise_h(0)
         regroup_weights("k", F, vcopy)
+        quantise_h(0)
         quantise_weights("k", F)
-        for q in range(BLOCKS):
-            zs[(0, F, q)] = weights_stationary(0, F, q)
         tanh_candidate(0)
-        for q in range(BLOCKS):
-            transposed_gate(0, F, q)
         transpose_h(1, 0, scopy)
         transpose_h(1, 1, scopy)
+        for q in range(BLOCKS):
+            zs[(0, F, q)] = weights_stationary(0, F, q)
+        for q in range(BLOCKS):
+            transposed_gate(0, F, q)
         regroup_weights("r", I, vcopy)
         regroup_weights("k", I, vcopy)
         quantise_weights("r", I)
         quantise_weights("k", I)
-        quantise_h(1)
         transpose_h(2, 0, scopy)
         transpose_h(2, 1, scopy)
         xz = input_term()
@@ -389,6 +392,7 @@ def tile_rlstmcell_pb_kernel(
             transposed_gate(0, I, q)
         regroup_weights("r", O, vcopy)
         add_input_bias(xz)
+        quantise_h(1)
         regroup_weights("k", O, vcopy)
         quantise_weights("r", O)
         quantise_weights("k", O)

@@ -323,9 +323,9 @@ def tile_rlstmcell_pb_kernel(
                 op=MULT,
             )
 
-        def new_cell(t, pair):
+        def new_cell(t, pair, engine=nc.gpsimd):
             cols = slice(2 * pair * P, (2 * pair + 2) * P)
-            nc.gpsimd.tensor_tensor(
+            engine.tensor_tensor(
                 out=c_new[t][:, :, cols], in0=kept[(t, pair)][:], in1=cand[t][:, :, cols], op=ADD
             )
 
@@ -434,6 +434,10 @@ def tile_rlstmcell_pb_kernel(
                 zs[(f // 4, F, f % 4)] = weights_stationary(f // 4, F, f % 4)
             if i < steps:
                 zs[(i // 4, I, i % 4)] = h_stationary(i // 4, i % 4)
+            if j == 12:
+                new_cell(GROUPS - 1, 0, nc.vector)
+            if j == 13:
+                new_cell(GROUPS - 1, 1, nc.vector)
             if j < steps:
                 transposed_gate(j // 4, O, j % 4)
             if f - 1 < steps:
@@ -471,7 +475,7 @@ def tile_rlstmcell_pb_kernel(
                     store_columns(out_0, t, h_new[t], slice(q * P, (q + 1) * P))
             if c - 1 < steps:
                 t, q = (c - 1) // 4, (c - 1) % 4
-                if q % 2 == 1:
+                if q % 2 == 1 and t * BLOCKS + q < steps - 4:
                     new_cell(t, q // 2)
             if i - 1 < steps and i % 2 == 0:
                 apply_input_gate((i - 1) // 4, (i - 1) % 4 // 2)

from contextlib import ExitStack

import concourse.mybir as mybir
from concourse.masks import make_identity

F32 = mybir.dt.float32
BF16 = mybir.dt.bfloat16
U32 = mybir.dt.uint32
U8 = mybir.dt.uint8
FP8X4 = mybir.dt.float8_e4m3fn_x4
SIGMOID = mybir.ActivationFunctionType.Sigmoid
TANH = mybir.ActivationFunctionType.Tanh
MULT = mybir.AluOpType.mult
ADD = mybir.AluOpType.add

P = 128
BATCH = 128
SLOTS = 16
D = 512
I, F, O = 0, 1, 2
GATES = 3
PACK = 4
HALVES = 2
GROUP = 4
GROUPS = SLOTS // GROUP
BLOCKS = D // P
MOVING = GROUP * BATCH

FLOPS = 2 * (BATCH + BATCH * SLOTS) * D * GATES * D


def tile_rlstmcell_pb_kernel(
    tc, inputs, h_state, c_state, c_upd, kernel, recurrent_kernel, bias, out_0, out_1
):
    nc = tc.nc
    with ExitStack() as ctx:
        const = ctx.enter_context(tc.tile_pool(name="const", bufs=1))
        resident = ctx.enter_context(tc.tile_pool(name="resident", bufs=1))
        loads = ctx.enter_context(tc.tile_pool(name="loads", bufs=3))
        stage = ctx.enter_context(tc.tile_pool(name="stage", bufs=2))
        gate_pool = ctx.enter_context(tc.tile_pool(name="gate_pool", bufs=2 * BLOCKS))
        block_pool = ctx.enter_context(tc.tile_pool(name="block_pool", bufs=BLOCKS))
        work = ctx.enter_context(tc.tile_pool(name="work", bufs=2))
        z_psum = ctx.enter_context(tc.psum_pool(name="z_psum", bufs=5))
        t_psum = ctx.enter_context(tc.psum_pool(name="t_psum", bufs=3))
        ctx.enter_context(tc.manual_schedule())

        weights = {"r": recurrent_kernel, "k": kernel}
        w_raw, h_sb, c_sb, cu_sb = {}, {}, {}, {}

        def load_weights(w, g):
            w_raw[(w, g)] = loads.tile([P, PACK, D], BF16, name="raw_" + w, bufs=2)
            nc.sync.dma_start(
                out=w_raw[(w, g)][:],
                in_=weights[w][:, g * D : (g + 1) * D].rearrange("(p t) c -> p t c", t=PACK),
            )

        def load_h(t):
            h_sb[t] = loads.tile([P, GROUP * D], BF16, name="h_rows", bufs=3)
            nc.sync.dma_start(out=h_sb[t][:], in_=h_state[:, t * GROUP * D : (t + 1) * GROUP * D])

        def load_candidate(t, first=0, count=GROUP):
            if first == 0:
                cu_sb[t] = loads.tile([P, GROUP, D], BF16, name="candidate_rows")
            slot = t * GROUP + first
            nc.sync.dma_start(
                out=cu_sb[t][:, first : first + count, :], in_=c_upd[:, slot : slot + count, :]
            )

        def load_cell(t):
            c_sb[t] = loads.tile([P, GROUP, D], BF16, name="cell_rows")
            nc.sync.dma_start(
                out=c_sb[t][:],
                in_=c_state[:, t * GROUP * D : (t + 1) * GROUP * D].rearrange(
                    "b (s d) -> b s d", s=GROUP
                ),
            )

        bias_rows = const.tile([P, P], BF16, name="bias_rows")
        nc.gpsimd.memset(bias_rows[:], 0.0)
        bias_row = const.tile([P, D], BF16, name="bias_row")
        nc.gpsimd.memset(bias_row[:], 0.0)
        ones = const.tile([P, P], BF16, name="ones")
        nc.gpsimd.memset(ones[:], 1.0)

        def load_biases():
            nc.sync.dma_start(
                out=bias_rows[0 : GATES * BLOCKS, :], in_=bias.rearrange("(m p) -> m p", p=P)
            )
            nc.sync.dma_start(out=bias_row[0:1, :], in_=bias[0:D].rearrange("(m p) -> m p", p=D))

        load_weights("r", F)
        x_sb = resident.tile([P, D], BF16, name="x_sb")
        nc.sync.dma_start(out=x_sb[:], in_=inputs)
        load_h(0)
        load_biases()
        load_weights("k", F)
        load_candidate(0)
        load_h(1)
        load_weights("r", I)
        load_weights("k", I)
        load_h(2)
        load_weights("r", O)
        load_weights("k", O)
        load_h(3)
        load_candidate(1)
        load_cell(0)
        load_candidate(2)
        load_cell(1)
        load_candidate(3)
        load_cell(2)
        load_cell(3)

        warm = const.tile([P, 1], F32, name="warm")
        nc.vector.memset(warm[:], 0.0)
        nc.scalar.activation(out=warm[:], in_=warm[:], func=SIGMOID)

        ident = const.tile([P, P], F32, name="ident")
        make_identity(nc, ident[:])
        ident_bf16 = const.tile([P, P], BF16, name="ident_bf16")
        nc.gpsimd.tensor_copy(out=ident_bf16[:], in_=ident[:])

        xT_codes = resident.tile([P, MOVING], U32, name="xT_codes", align_bytes=64)
        xT_scales = resident.tile([P, MOVING], U8, name="xT_scales", align_bytes=64)
        xT_grouped = resident.tile([P, BATCH * PACK], BF16, name="xT_grouped", align_bytes=64)

        def transpose_x():
            xT_ps = t_psum.tile([P, MOVING], F32, name="xT_ps", tag="t")
            x_words = x_sb[:].bitcast(F32)
            for u in range(HALVES):
                nc.tensor.transpose(
                    xT_ps[:, u * P : (u + 1) * P], x_words[:, u : HALVES * P : HALVES], ident[:]
                )
            nc.scalar.copy(
                out=xT_grouped[:].bitcast(F32).rearrange("p (b u) -> p b u", u=HALVES),
                in_=xT_ps[:, 0 : HALVES * P].rearrange("p (u b) -> p b u", u=HALVES),
            )

        def quantise_x(s):
            cols = slice(s * BATCH, (s + 1) * BATCH)
            nc.vector.quantize_mx(
                out=xT_codes[:, cols].bitcast(FP8X4), scales=xT_scales[:, cols], in_=xT_grouped[:]
            )

        bias_cols = const.tile([P, GATES * BLOCKS], F32, name="bias_cols")
        bias_i = const.tile([P, D], F32, name="bias_i")

        def biases_to_columns():
            bias_ps = t_psum.tile([P, MOVING], F32, name="bias_ps", tag="t")
            nc.tensor.matmul(
                bias_ps[:, 0:P], lhsT=bias_rows[:], rhs=ident_bf16[:], start=True, stop=True
            )
            nc.scalar.copy(out=bias_cols[:], in_=bias_ps[:, 0 : GATES * BLOCKS])

        def spread_input_bias():
            spread = t_psum.tile([P, D], F32, name="spread", tag="t")
            nc.tensor.matmul(spread[:], lhsT=ones[:], rhs=bias_row[:], start=True, stop=True)
            nc.scalar.copy(out=bias_i[:], in_=spread[:])

        hT_grouped, hT_codes, hT_scales = {}, {}, {}

        def transpose_h(t, pair, copy):
            if pair == 0:
                hT_grouped[t] = stage.tile(
                    [P, MOVING * PACK], BF16, name="hT_grouped", align_bytes=64
                )
            h_words = h_sb[t][:].bitcast(F32)
            hT_ps = t_psum.tile([P, MOVING], F32, name="hT_ps", tag="t")
            for u in range(HALVES):
                for j in range(2):
                    slot = (2 * pair + j) * HALVES * P
                    nc.tensor.transpose(
                        hT_ps[:, (2 * u + j) * P : (2 * u + j + 1) * P],
                        h_words[:, slot + u : slot + HALVES * P : HALVES],
                        ident[:],
                    )
            copy(
                out=hT_grouped[t][:]
                .bitcast(F32)[:, pair * MOVING : (pair + 1) * MOVING]
                .rearrange("p (c u) -> p c u", u=HALVES),
                in_=hT_ps[:].rearrange("p (u c) -> p c u", u=HALVES),
            )

        def quantise_h(t):
            hT_codes[t] = stage.tile([P, MOVING], U32, name="hT_codes", bufs=GROUPS, align_bytes=64)
            hT_scales[t] = stage.tile([P, MOVING], U8, name="hT_scales", bufs=GROUPS, align_bytes=64)
            nc.vector.quantize_mx(
                out=hT_codes[t][:].bitcast(FP8X4), scales=hT_scales[t][:], in_=hT_grouped[t][:]
            )

        w_grouped = {}
        w_codes = {w: resident.tile([P, GATES * D], U32, name="codes_" + w, align_bytes=64) for w in weights}
        w_scales = {w: resident.tile([P, GATES * D], U8, name="scales_" + w, align_bytes=64) for w in weights}

        def regroup_weights(w, g, copy):
            w_grouped[w] = stage.tile([P, D, PACK], BF16, name="grouped_" + w, bufs=1, align_bytes=64)
            copy(
                out=w_grouped[w][:].rearrange("p (c i) t -> p c t i", i=4),
                in_=w_raw[(w, g)][:].rearrange("p t (c i) -> p c t i", i=4),
            )

        def quantise_weights(w, g):
            nc.vector.quantize_mx(
                out=w_codes[w][:, g * D : (g + 1) * D].bitcast(FP8X4),
                scales=w_scales[w][:, g * D : (g + 1) * D],
                in_=w_grouped[w][:].rearrange("p c t -> p (c t)"),
            )

        def h_stationary(t, s):
            z = z_psum.tile([P, D], F32, name="z")
            rows = slice(s * BATCH, (s + 1) * BATCH)
            nc.tensor.matmul_mx(
                out=z[:],
                lhsT=hT_codes[t][:, rows].bitcast(FP8X4),
                lhsT_scale=hT_scales[t][:, rows],
                rhs=w_codes["r"][:, I * D : (I + 1) * D].bitcast(FP8X4),
                rhs_scale=w_scales["r"][:, I * D : (I + 1) * D],
                start=True,
                stop=True,
            )
            return z

        xz_i = const.tile([P, D], F32, name="xz_i")

        def input_term():
            z = z_psum.tile([P, D], F32, name="z")
            nc.tensor.matmul_mx(
                out=z[:],
                lhsT=xT_codes[:, 0:BATCH].bitcast(FP8X4),
                lhsT_scale=xT_scales[:, 0:BATCH],
                rhs=w_codes["k"][:, I * D : (I + 1) * D].bitcast(FP8X4),
                rhs_scale=w_scales["k"][:, I * D : (I + 1) * D],
                start=True,
                stop=True,
            )
            return z

        def add_input_bias(z):
            nc.vector.tensor_tensor(out=xz_i[:], in0=z[:], in1=bias_i[:], op=ADD)

        def weights_stationary(t, g, q):
            cols = slice((g * BLOCKS + q) * P, (g * BLOCKS + q + 1) * P)
            z = z_psum.tile([P, MOVING], F32, name="z")
            nc.tensor.matmul_mx(
                out=z[:],
                lhsT=w_codes["r"][:, cols].bitcast(FP8X4),
                lhsT_scale=w_scales["r"][:, cols],
                rhs=hT_codes[t][:].bitcast(FP8X4),
                rhs_scale=hT_scales[t][:],
                start=True,
                stop=False,
            )
            nc.tensor.matmul_mx(
                out=z[:],
                lhsT=w_codes["k"][:, cols].bitcast(FP8X4),
                lhsT_scale=w_scales["k"][:, cols],
                rhs=xT_codes[:].bitcast(FP8X4),
                rhs_scale=xT_scales[:],
                start=False,
                stop=True,
            )
            return z

        def block(tile3, q):
            return tile3[:, :, q * P : (q + 1) * P]

        cand, c_new, h_new, gate_i, tanh_c, kept = {}, {}, {}, {}, {}, {}

        def tanh_candidate(t, first=0, count=GROUP):
            if first == 0:
                cand[t] = work.tile([P, GROUP, D], F32, name="cand", bufs=4)
            part = slice(first, first + count)
            nc.scalar.activation(out=cand[t][:, part, :], in_=cu_sb[t][:, part, :], func=TANH)

        def input_preactivation(t, s):
            if s % 2 == 0:
                gate_i[(t, s // 2)] = gate_pool.tile([P, 2, D], F32, name="gate_i", bufs=3)
            nc.vector.tensor_tensor(
                out=gate_i[(t, s // 2)][:, s % 2, :], in0=zs[(t, I, s)][:], in1=xz_i[:], op=ADD
            )

        def input_gate(t, s):
            gate = gate_i[(t, s // 2)][:, s % 2, :]
            nc.scalar.activation(out=gate, in_=gate, func=SIGMOID)

        def apply_input_gate(t, pair):
            part = cand[t][:, 2 * pair : 2 * pair + 2, :]
            nc.gpsimd.tensor_tensor(out=part, in0=gate_i[(t, pair)][:], in1=part, op=MULT)

        def apply_transposed_input_gate(t, q):
            nc.vector.tensor_tensor(
                out=block(cand[t], q), in0=gates[(t, I, q)], in1=block(cand[t], q), op=MULT
            )

        def transposed_gate(t, g, q):
            gatesT[(t, g, q)] = gate_pool.tile([P, MOVING], F32, name="gateT", bufs=3 * BLOCKS)
            m = g * BLOCKS + q
            nc.scalar.activation(
                out=gatesT[(t, g, q)][:],
                in_=zs[(t, g, q)][:],
                func=SIGMOID,
                bias=bias_cols[:, m : m + 1],
                scale=1.0,
            )

        def to_batch_rows(t, g, q):
            gate = t_psum.tile([P, GROUP * P], F32, name="gate", tag="t")
            for s in range(GROUP):
                nc.tensor.transpose(
                    gate[:, s * P : (s + 1) * P], gatesT[(t, g, q)][:, s * P : (s + 1) * P], ident[:]
                )
            gates[(t, g, q)] = gate[:].rearrange("b (s d) -> b s d", s=GROUP)

        def apply_forget_gate(t, q):
            if q == 0:
                c_new[t] = work.tile([P, GROUP, D], F32, name="c_new", bufs=3)
            if q % 2 == 0:
                kept[(t, q // 2)] = block_pool.tile([P, GROUP, 2 * P], F32, name="kept", bufs=3)
            nc.vector.tensor_tensor(
                out=block(kept[(t, q // 2)], q % 2),
                in0=gates[(t, F, q)],
                in1=block(c_sb[t], q),
                op=MULT,
            )

        def new_cell(t, pair, engine=nc.gpsimd):
            cols = slice(2 * pair * P, (2 * pair + 2) * P)
            engine.tensor_tensor(
                out=c_new[t][:, :, cols], in0=kept[(t, pair)][:], in1=cand[t][:, :, cols], op=ADD
            )

        def tanh_cell(t, q):
            tanh_c[(t, q)] = block_pool.tile([P, GROUP, P], F32, name="tanh_c")
            nc.scalar.activation(out=tanh_c[(t, q)][:], in_=block(c_new[t], q), func=TANH)

        def new_h(t, q):
            if q == 0:
                h_new[t] = work.tile([P, GROUP, D], F32, name="h_new")
            nc.vector.tensor_tensor(
                out=block(h_new[t], q), in0=gates[(t, O, q)], in1=tanh_c[(t, q)][:], op=MULT
            )

        def store_columns(out, t, tile3, cols):
            nc.sync.dma_start(
                out=out[:, t * GROUP * D : (t + 1) * GROUP * D].rearrange(
                    "b (s d) -> b s d", s=GROUP
                )[:, :, cols],
                in_=tile3[:, :, cols],
            )

        def store_pair(out, t, pair, tile3):
            store_columns(out, t, tile3, slice(2 * pair * P, (2 * pair + 2) * P))

        def store(out, t, tile3):
            nc.sync.dma_start(
                out=out[:, t * GROUP * D : (t + 1) * GROUP * D],
                in_=tile3[:].rearrange("b s d -> b (s d)"),
            )

        zs, gatesT, gates = {}, {}, {}

        vcopy, scopy = nc.vector.tensor_copy, nc.scalar.copy
        transpose_x()
        transpose_h(0, 0, scopy)
        transpose_h(0, 1, scopy)
        biases_to_columns()
        spread_input_bias()
        regroup_weights("r", F, vcopy)
        for s in range(GROUP):
            quantise_x(s)
        quantise_weights("r", F)
        regroup_weights("k", F, vcopy)
        quantise_h(0)
        quantise_weights("k", F)
        tanh_candidate(0)
        transpose_h(1, 0, scopy)
        transpose_h(1, 1, scopy)
        for q in range(BLOCKS):
            zs[(0, F, q)] = weights_stationary(0, F, q)
        for q in range(BLOCKS):
            transposed_gate(0, F, q)
        regroup_weights("r", I, vcopy)
        regroup_weights("k", I, vcopy)
        quantise_weights("r", I)
        quantise_weights("k", I)
        transpose_h(2, 0, scopy)
        transpose_h(2, 1, scopy)
        xz = input_term()
        for q in range(BLOCKS):
            zs[(0, I, q)] = weights_stationary(0, I, q)
        for q in range(BLOCKS):
            transposed_gate(0, I, q)
        regroup_weights("r", O, vcopy)
        add_input_bias(xz)
        quantise_h(1)
        regroup_weights("k", O, vcopy)
        quantise_weights("r", O)
        quantise_weights("k", O)
        quantise_h(2)
        for q in range(BLOCKS):
            zs[(1, F, q)] = weights_stationary(1, F, q)
            transposed_gate(1, F, q)
        for q in range(BLOCKS):
            to_batch_rows(0, I, q)
            apply_transposed_input_gate(0, q)
        tanh_candidate(1)
        for q in range(BLOCKS):
            to_batch_rows(0, F, q)
            apply_forget_gate(0, q)
            if q % 2 == 1:
                new_cell(0, q // 2)
        for s in range(GROUP):
            zs[(1, I, s)] = h_stationary(1, s)
            input_preactivation(1, s)
        tanh_candidate(2)
        for s in range(GROUP):
            input_gate(1, s)
            if s % 2 == 1:
                apply_input_gate(1, s // 2)
        zs[(0, O, 0)] = weights_stationary(0, O, 0)
        zs[(2, F, 0)] = weights_stationary(2, F, 0)
        zs[(2, I, 0)] = h_stationary(2, 0)
        to_batch_rows(1, F, 0)
        input_preactivation(2, 0)
        apply_forget_gate(1, 0)
        store_pair(out_1, 0, 0, c_new[0])

        steps = SLOTS
        for j in range(steps + 1):
            o, f, i, c = j + 1, j + 9, j + 9, j + 5
            if o < steps:
                zs[(o // 4, O, o % 4)] = weights_stationary(o // 4, O, o % 4)
            if f < steps:
                zs[(f // 4, F, f % 4)] = weights_stationary(f // 4, F, f % 4)
            if i < steps:
                zs[(i // 4, I, i % 4)] = h_stationary(i // 4, i % 4)
            if j == 12:
                new_cell(GROUPS - 1, 0, nc.vector)
            if j == 13:
                new_cell(GROUPS - 1, 1, nc.vector)
            if j < steps:
                transposed_gate(j // 4, O, j % 4)
            if f - 1 < steps:
                transposed_gate((f - 1) // 4, F, (f - 1) % 4)
            if i - 1 < steps:
                input_gate((i - 1) // 4, (i - 1) % 4)
            if j < steps:
                tanh_cell(j // 4, j % 4)
            if j == 2:
                tanh_candidate(3)
            if j == 0:
                transpose_h(3, 0, vcopy)
            if j == 1:
                transpose_h(3, 1, vcopy)
            if c < steps:
                to_batch_rows(c // 4, F, c % 4)
            if j > 0:
                to_batch_rows((j - 1) // 4, O, (j - 1) % 4)
            if i < steps:
                input_preactivation(i // 4, i % 4)
            if j == 1:
                quantise_h(3)
            if c < steps:
                apply_forget_gate(c // 4, c % 4)
            if j > 0:
                t, q = (j - 1) // 4, (j - 1) % 4
                new_h(t, q)
                if q % 2 == 1:
                    n = j - 1 + 2 * 1
                    if n < steps:
                        store_pair(out_1, n // 4, n % 4 // 2, c_new[n // 4])
                if q % 2 == 1 and j < steps - 1:
                    store_pair(out_0, t, q // 2, h_new[t])
                if j > steps - 2:
                    store_columns(out_0, t, h_new[t], slice(q * P, (q + 1) * P))
            if c - 1 < steps:
                t, q = (c - 1) // 4, (c - 1) % 4
                if q % 2 == 1 and t * BLOCKS + q < steps - 4:
                    new_cell(t, q // 2)
            if i - 1 < steps and i % 2 == 0:
                apply_input_gate((i - 1) // 4, (i - 1) % 4 // 2)
